import numpy as np
import ml_dtypes


def mxq(x, axis, fmt="e4m3"):
    dtype, down = {"e4m3": (ml_dtypes.float8_e4m3fn, 7), "e5m2": (ml_dtypes.float8_e5m2, 14)}[fmt]
    v = np.moveaxis(np.asarray(x, np.float32).astype(ml_dtypes.bfloat16).astype(np.float64), axis, -1)
    blocks = v.reshape(v.shape[:-1] + (-1, 32))
    amax = np.abs(blocks).max(-1, keepdims=True)
    byte = np.maximum(np.where(amax > 0, np.frexp(amax)[1] - 1 + 127, 0) - down, 1)
    scale = np.exp2(byte - 127.0)
    codes = (blocks / scale).astype(np.float32).astype(dtype).astype(np.float64)
    return np.moveaxis((codes * scale).reshape(v.shape), -1, axis)


WIDE = False


def mx_kscale(k):
    if not WIDE:
        return np.ones(k)
    levels = np.array([10, -10, 5, -5, 0])
    if k % 512:
        return np.exp2(np.random.permutation(np.resize(levels, k // 32))).repeat(32)
    a = np.empty((k // 512, 16))
    for p in range(k // 512):
        a[p, :8] = np.random.permutation(np.resize(levels, 8))
        for g in range(8):
            far = levels[np.abs(levels - a[p, g]) >= 10]
            a[p, g + 8] = far[np.random.randint(len(far))]
    return np.exp2(a.ravel()).repeat(32)


BF16 = ml_dtypes.bfloat16


def bf(x):
    return np.asarray(x, np.float32).astype(BF16)


def f64(x):
    return np.asarray(x).astype(np.float64)


B, S, M, D, H = 32, 128, 3, 512, 512


def setup_inputs():
    s = mx_kscale(2 * D)
    lens = np.random.randint(0, M + 1, (B, S))
    valid = (np.arange(M)[None, None, :] < lens[:, :, None]).astype(np.float64)
    src = np.random.standard_normal((B, S, M, D)) / np.sqrt(M) * s[:D]
    neigh = np.random.standard_normal((B, S, M, D)) * 2.0 * valid[..., None] * s[D:]
    return {"src_node_features": bf(src), "neigh_node_features": bf(neigh),
            "W_map": bf(np.random.standard_normal((2 * D, H)) / np.sqrt(2 * D) / s[:, None]),
            "b_map": bf(-0.5 + 0.3 * np.random.standard_normal(H))}


def reference(src_node_features, neigh_node_features, W_map, b_map):
    src, neigh = f64(src_node_features), f64(neigh_node_features)
    valid = np.any(neigh != 0, axis=-1)
    num = np.sum(valid, axis=-1).astype(np.float64)
    neigh_mean = neigh.sum(axis=2) / np.maximum(num, 1.0)[..., None]
    hidden = np.concatenate([src.sum(axis=2), neigh_mean], axis=-1)
    hidden = hidden.reshape(-1, hidden.shape[-1])
    v = (mxq(hidden, 1, "e4m3") @ mxq(f64(W_map), 0, "e4m3")) + f64(b_map)
    return np.where(v >= 0, v, 0.01 * v)

@@ -1,0 +1,206 @@
+import concourse.mybir as mybir
+from concourse.masks import make_identity
+
+F32 = mybir.dt.float32
+BF16 = mybir.dt.bfloat16
+U32 = mybir.dt.uint32
+U8 = mybir.dt.uint8
+FP8X4 = mybir.dt.float8_e4m3fn_x4
+ALU = mybir.AluOpType
+ACT = mybir.ActivationFunctionType
+AXIS = mybir.AxisListType
+
+P = 128
+SLOTS = 3
+D = 512
+H = 512
+K = 2 * D
+NODES = 4096
+K_PASS = 512
+PASSES = K // K_PASS
+NODE_TILES = NODES // P
+PAIR = 2
+N_PAIRS = NODE_TILES // PAIR
+PREFETCH = 3
+SLOPE = 0.01
+
+FLOPS = 2 * NODES * K * H
+
+
+def tile_syntacticgcn_t_kernel(tc, src_node_features, neigh_node_features, W_map, b_map, out):
+    nc = tc.nc
+
+    src_v = src_node_features.rearrange("b (q t) m d -> (b q) t (m d)", t=NODE_TILES)
+    neigh_v = neigh_node_features.rearrange("b (q t) m d -> (b q) t (m d)", t=NODE_TILES)
+    out_v = out.rearrange("(p t) h -> p t h", t=NODE_TILES)
+
+    with tc.tile_pool(name="const", bufs=1) as const, tc.tile_pool(name="data", bufs=PREFETCH + 1) as data, tc.tile_pool(
+        name="work", bufs=2
+    ) as work, tc.tile_pool(name="junk", bufs=4) as junk_pool, tc.psum_pool(name="psum", bufs=4) as psum:
+        w_raw = const.tile([P, PASSES * 4 * H], BF16)
+        nc.sync.dma_start(
+            out=w_raw[:].rearrange("p (g th) -> p g th", g=PASSES),
+            in_=W_map.rearrange("(g q t) h -> q g (t h)", g=PASSES, t=4),
+        )
+        ident = const.tile([P, P], F32)
+        make_identity(nc, ident[:])
+
+        xs_of = {}
+        xn_of = {}
+
+        def load(c):
+            xn = data.tile([P, PAIR, SLOTS * D], BF16)
+            nc.sync.dma_start(out=xn[:], in_=neigh_v[:, PAIR * c : PAIR * (c + 1), :])
+            xs = data.tile([P, PAIR, SLOTS * D], BF16)
+            nc.sync.dma_start(out=xs[:], in_=src_v[:, PAIR * c : PAIR * (c + 1), :])
+            xn_of[c] = xn
+            xs_of[c] = xs
+
+        for c in range(PREFETCH):
+            load(c)
+        bias_bf = const.tile([P, H], BF16)
+        nc.sync.dma_start(out=bias_bf[:], in_=b_map.partition_broadcast(P))
+
+        w_grouped = const.tile([P, PASSES * H * 4], BF16, align_bytes=64)
+        w_codes = const.tile([P, PASSES * H], U32, align_bytes=64)
+        w_scales = const.tile([P, PASSES * H], U8, align_bytes=64)
+        for g in range(PASSES):
+            nc.vector.tensor_copy(
+                out=w_grouped[:, g * 4 * H : (g + 1) * 4 * H].rearrange("p (h t) -> p h t", t=4),
+                in_=w_raw[:, g * 4 * H : (g + 1) * 4 * H].rearrange("p (t h) -> p h t", t=4),
+            )
+        for g in range(PASSES):
+            nc.vector.quantize_mx(
+                out=w_codes[:, g * H : (g + 1) * H].bitcast(FP8X4),
+                scales=w_scales[:, g * H : (g + 1) * H],
+                in_=w_grouped[:, g * 4 * H : (g + 1) * 4 * H],
+            )
+        bias = const.tile([P, H], F32)
+        nc.vector.tensor_copy(out=bias[:], in_=bias_bf[:])
+
+        abs_sum_of = {}
+        recip_of = {}
+        hid_of = {}
+        nsum_of = {}
+        xt_of = {}
+        grouped_of = {}
+        acc_of = {}
+
+        def count(c):
+            abs_sum = work.tile([P, PAIR * SLOTS], F32)
+            for j in range(PAIR):
+                for s in range(SLOTS):
+                    junk = junk_pool.tile([P, D], BF16)
+                    nc.scalar.activation(
+                        out=junk[:],
+                        in_=xn_of[c][:, j, s * D : (s + 1) * D],
+                        func=ACT.Abs,
+                        accum_out=abs_sum[:, j * SLOTS + s : j * SLOTS + s + 1],
+                    )
+            abs_sum_of[c] = abs_sum
+
+        def reciprocal_count(c):
+            valid = work.tile([P, PAIR, SLOTS], F32)
+            nc.vector.tensor_scalar(
+                out=valid[:].rearrange("p j s -> p (j s)"), in0=abs_sum_of[c][:], scalar1=0.0, scalar2=None, op0=ALU.is_gt
+            )
+            num = work.tile([P, PAIR], F32)
+            nc.vector.tensor_reduce(out=num[:], in_=valid[:], axis=AXIS.X, op=ALU.add)
+            den = work.tile([P, PAIR], F32)
+            nc.vector.tensor_scalar_max(den[:], num[:], 1.0)
+            recip = work.tile([P, PAIR], F32)
+            nc.vector.reciprocal(recip[:], den[:])
+            recip_of[c] = recip
+
+        def sums(c):
+            xs = xs_of[c]
+            xn = xn_of[c]
+            hid = work.tile([P, PAIR, K], BF16)
+            s01 = work.tile([P, PAIR, D], F32)
+            n01 = work.tile([P, PAIR, D], F32)
+            nsum = work.tile([P, PAIR, D], F32)
+            nc.vector.tensor_tensor(out=s01[:], in0=xs[:, :, 0:D], in1=xs[:, :, D : 2 * D], op=ALU.add)
+            nc.vector.tensor_tensor(out=n01[:], in0=xn[:, :, 0:D], in1=xn[:, :, D : 2 * D], op=ALU.add)
+            nc.vector.tensor_tensor(out=hid[:, :, 0:D], in0=s01[:], in1=xs[:, :, 2 * D : 3 * D], op=ALU.add)
+            nc.vector.tensor_tensor(out=nsum[:], in0=n01[:], in1=xn[:, :, 2 * D : 3 * D], op=ALU.add)
+            hid_of[c] = hid
+            nsum_of[c] = nsum
+
+        def scale(c):
+            for j in range(PAIR):
+                nc.scalar.activation(
+                    out=hid_of[c][:, j, D:K], in_=nsum_of[c][:, j, :], func=ACT.Copy, scale=recip_of[c][:, j : j + 1]
+                )
+
+        def transpose(c):
+            words = hid_of[c][:].rearrange("p j k -> p (j k)").bitcast(F32)
+            xts = []
+            for j in range(PAIR):
+                xt = psum.tile([P, 2 * PASSES, P], F32)
+                for cu in range(2 * PASSES):
+                    g, u = divmod(cu, 2)
+                    first = j * (K // 2) + g * 2 * P
+                    nc.tensor.transpose(xt[:, cu, :], words[:, first + u : first + 2 * P : 2], ident[:])
+                xts.append(xt)
+            xt_of[c] = xts
+
+        def regroup(c):
+            grouped = work.tile([P, PAIR * K], BF16, align_bytes=64)
+            grouped_w = grouped[:].bitcast(F32).rearrange("p (j g n u) -> p j g n u", j=PAIR, g=PASSES, u=2)
+            for j in range(PAIR):
+                nc.scalar.copy(out=grouped_w[:, j], in_=xt_of[c][j][:].rearrange("p (g u) n -> p g n u", u=2))
+            grouped_of[c] = grouped
+
+        def quantise_and_multiply(c):
+            codes = work.tile([P, PAIR * PASSES * P], U32, align_bytes=64)
+            scales = work.tile([P, PAIR * PASSES * P], U8, align_bytes=64)
+            nc.vector.quantize_mx(out=codes[:].bitcast(FP8X4), scales=scales[:], in_=grouped_of[c][:])
+            accs = []
+            for j in range(PAIR):
+                acc = psum.tile([P, H], F32)
+                for g in range(PASSES):
+                    cols = slice((j * PASSES + g) * P, (j * PASSES + g + 1) * P)
+                    nc.tensor.matmul_mx(
+                        out=acc[:],
+                        lhsT=codes[:, cols].bitcast(FP8X4),
+                        lhsT_scale=scales[:, cols],
+                        rhs=w_codes[:, g * H : (g + 1) * H].bitcast(FP8X4),
+                        rhs_scale=w_scales[:, g * H : (g + 1) * H],
+                        start=(g == 0),
+                        stop=(g == PASSES - 1),
+                    )
+                accs.append(acc)
+            acc_of[c] = accs
+
+        def finish(c):
+            biased = work.tile([P, PAIR, H], F32)
+            result = work.tile([P, PAIR, H], F32)
+            for j in range(PAIR):
+                nc.vector.tensor_tensor(out=biased[:, j, :], in0=acc_of[c][j][:], in1=bias[:], op=ALU.add)
+            for j in range(PAIR):
+                nc.vector.scalar_tensor_tensor(
+                    out=result[:, j, :], in0=biased[:, j, :], scalar=SLOPE, in1=biased[:, j, :], op0=ALU.mult, op1=ALU.max
+                )
+            nc.sync.dma_start(out=out_v[:, PAIR * c : PAIR * (c + 1), :], in_=result[:])
+
+        count(0)
+        reciprocal_count(0)
+        for i in range(N_PAIRS + 2):
+            if i + PREFETCH < N_PAIRS:
+                load(i + PREFETCH)
+            if i + 1 < N_PAIRS:
+                count(i + 1)
+            if i < N_PAIRS:
+                sums(i)
+            if i + 1 < N_PAIRS:
+                reciprocal_count(i + 1)
+            if 0 <= i - 1 < N_PAIRS:
+                regroup(i - 1)
+            if i < N_PAIRS:
+                scale(i)
+            if 0 <= i - 2:
+                finish(i - 2)
+            if 0 <= i - 1 < N_PAIRS:
+                quantise_and_multiply(i - 1)
+            if i < N_PAIRS:
+                transpose(i)

@@ -8,7 +8,6 @@ U8 = mybir.dt.uint8
 FP8X4 = mybir.dt.float8_e4m3fn_x4
 ALU = mybir.AluOpType
 ACT = mybir.ActivationFunctionType
-AXIS = mybir.AxisListType
 
 P = 128
 SLOTS = 3
@@ -18,11 +17,15 @@ K = 2 * D
 NODES = 4096
 K_PASS = 512
 PASSES = K // K_PASS
+PACK = 4
 NODE_TILES = NODES // P
 PAIR = 2
 N_PAIRS = NODE_TILES // PAIR
-PREFETCH = 3
+PREFETCH = 4
 SLOPE = 0.01
+ROW_TILES = SLOTS
+WIN = 44
+WIN_STEP = 42
 
 FLOPS = 2 * NODES * K * H
 
@@ -30,44 +33,72 @@ FLOPS = 2 * NODES * K * H
 def tile_syntacticgcn_t_kernel(tc, src_node_features, neigh_node_features, W_map, b_map, out):
     nc = tc.nc
 
-    src_v = src_node_features.rearrange("b (q t) m d -> (b q) t (m d)", t=NODE_TILES)
-    neigh_v = neigh_node_features.rearrange("b (q t) m d -> (b q) t (m d)", t=NODE_TILES)
-    out_v = out.rearrange("(p t) h -> p t h", t=NODE_TILES)
+    src_v = src_node_features.rearrange("b q m d -> (b q) (m d)").rearrange("(c j p) x -> c p j x", j=PAIR, p=P)
+    neigh_v = neigh_node_features.rearrange("b q m d -> (b q) (m d)").rearrange("(c j p) x -> c p j x", j=PAIR, p=P)
+    rows_v = neigh_node_features.rearrange("b q m d -> (b q m) d").rearrange("(c k p) d -> c p k d", k=PAIR * ROW_TILES, p=P)
+    out_v = out.rearrange("(c j p) h -> c p j h", j=PAIR, p=P)
+
+    def by_rows(c):
+        return c % 4 != 2
 
     with tc.tile_pool(name="const", bufs=1) as const, tc.tile_pool(name="data", bufs=PREFETCH + 1) as data, tc.tile_pool(
         name="work", bufs=2
-    ) as work, tc.tile_pool(name="junk", bufs=4) as junk_pool, tc.psum_pool(name="psum", bufs=4) as psum:
-        w_raw = const.tile([P, PASSES * 4 * H], BF16)
-        nc.sync.dma_start(
-            out=w_raw[:].rearrange("p (g th) -> p g th", g=PASSES),
-            in_=W_map.rearrange("(g q t) h -> q g (t h)", g=PASSES, t=4),
-        )
-        ident = const.tile([P, P], F32)
-        make_identity(nc, ident[:])
-
+    ) as work, tc.tile_pool(name="small", bufs=3) as small, tc.tile_pool(name="junk", bufs=4) as junk_pool, tc.psum_pool(
+        name="psum_x", bufs=2
+    ) as psum_x, tc.psum_pool(name="psum_acc", bufs=3) as psum_acc, tc.psum_pool(name="psum_num", bufs=1) as psum_num:
         xs_of = {}
         xn_of = {}
 
         def load(c):
-            xn = data.tile([P, PAIR, SLOTS * D], BF16)
-            nc.sync.dma_start(out=xn[:], in_=neigh_v[:, PAIR * c : PAIR * (c + 1), :])
+            xn = data.tile([P, PAIR * SLOTS, D], BF16)
+            if by_rows(c):
+                nc.sync.dma_start(out=xn[:], in_=rows_v[c])
+            else:
+                nc.sync.dma_start(out=xn[:].rearrange("p (j s) d -> p j (s d)", j=PAIR), in_=neigh_v[c])
             xs = data.tile([P, PAIR, SLOTS * D], BF16)
-            nc.sync.dma_start(out=xs[:], in_=src_v[:, PAIR * c : PAIR * (c + 1), :])
+            nc.sync.dma_start(out=xs[:], in_=src_v[c])
             xn_of[c] = xn
             xs_of[c] = xs
 
-        for c in range(PREFETCH):
+        load(0)
+        w_raw = const.tile([P, PASSES * PACK * H], BF16)
+        nc.sync.dma_start(
+            out=w_raw[:].rearrange("p (g th) -> p g th", g=PASSES),
+            in_=W_map.rearrange("(g q t) h -> q g (t h)", g=PASSES, t=PACK),
+        )
+        for c in range(1, PREFETCH):
             load(c)
         bias_bf = const.tile([P, H], BF16)
         nc.sync.dma_start(out=bias_bf[:], in_=b_map.partition_broadcast(P))
 
-        w_grouped = const.tile([P, PASSES * H * 4], BF16, align_bytes=64)
+        same_node = const.tile([P, ROW_TILES, P, SLOTS], BF16)
+        nc.gpsimd.memset(same_node[:], 1.0)
+        for j in range(ROW_TILES):
+            for low in (True, False):
+                sign = 1 if low else -1
+                nc.gpsimd.affine_select(
+                    out=same_node[:, j],
+                    in_=same_node[:, j],
+                    pattern=[[-SLOTS * sign, P], [0, SLOTS]],
+                    compare_op=ALU.is_ge,
+                    fill=0.0,
+                    base=P * j * sign + (0 if low else SLOTS - 1),
+                    channel_multiplier=sign,
+                )
+        window = const.tile([P, PAIR, ROW_TILES, WIN], BF16)
+        for jj in range(PAIR):
+            for j in range(ROW_TILES):
+                nc.gpsimd.tensor_copy(out=window[:, jj, j, :], in_=same_node[:, j, WIN_STEP * j : WIN_STEP * j + WIN, 0])
+        ident = const.tile([P, P], F32)
+        make_identity(nc, ident[:])
+
+        w_grouped = const.tile([P, PASSES * H * PACK], BF16, align_bytes=64)
         w_codes = const.tile([P, PASSES * H], U32, align_bytes=64)
         w_scales = const.tile([P, PASSES * H], U8, align_bytes=64)
         for g in range(PASSES):
             nc.vector.tensor_copy(
-                out=w_grouped[:, g * 4 * H : (g + 1) * 4 * H].rearrange("p (h t) -> p h t", t=4),
-                in_=w_raw[:, g * 4 * H : (g + 1) * 4 * H].rearrange("p (t h) -> p h t", t=4),
+                out=w_grouped[:, g * 4 * H : (g + 1) * 4 * H].rearrange("p (h t) -> p h t", t=PACK),
+                in_=w_raw[:, g * 4 * H : (g + 1) * 4 * H].rearrange("p (t h) -> p h t", t=PACK),
             )
         for g in range(PASSES):
             nc.vector.quantize_mx(
@@ -79,76 +110,167 @@ def tile_syntacticgcn_t_kernel(tc, src_node_features, neigh_node_features, W_map
         nc.vector.tensor_copy(out=bias[:], in_=bias_bf[:])
 
         abs_sum_of = {}
-        recip_of = {}
-        hid_of = {}
+        factor_of = {}
+        select_of = {}
+        hid_src_of = {}
         nsum_of = {}
+        hid_neigh_of = {}
         xt_of = {}
+        nt_of = {}
         grouped_of = {}
         acc_of = {}
 
         def count(c):
-            abs_sum = work.tile([P, PAIR * SLOTS], F32)
-            for j in range(PAIR):
-                for s in range(SLOTS):
-                    junk = junk_pool.tile([P, D], BF16)
-                    nc.scalar.activation(
-                        out=junk[:],
-                        in_=xn_of[c][:, j, s * D : (s + 1) * D],
-                        func=ACT.Abs,
-                        accum_out=abs_sum[:, j * SLOTS + s : j * SLOTS + s + 1],
-                    )
+            abs_sum = small.tile([P, PAIR * SLOTS], F32)
+            for k in range(PAIR * SLOTS):
+                junk = junk_pool.tile([P, D], BF16)
+                nc.scalar.activation(
+                    out=junk[:], in_=xn_of[c][:, k, :], func=ACT.Abs, accum_out=abs_sum[:, k : k + 1]
+                )
             abs_sum_of[c] = abs_sum
 
-        def reciprocal_count(c):
-            valid = work.tile([P, PAIR, SLOTS], F32)
-            nc.vector.tensor_scalar(
-                out=valid[:].rearrange("p j s -> p (j s)"), in0=abs_sum_of[c][:], scalar1=0.0, scalar2=None, op0=ALU.is_gt
-            )
-            num = work.tile([P, PAIR], F32)
-            nc.vector.tensor_reduce(out=num[:], in_=valid[:], axis=AXIS.X, op=ALU.add)
-            den = work.tile([P, PAIR], F32)
-            nc.vector.tensor_scalar_max(den[:], num[:], 1.0)
-            recip = work.tile([P, PAIR], F32)
-            nc.vector.reciprocal(recip[:], den[:])
-            recip_of[c] = recip
+        def factor(c):
+            if by_rows(c):
+                flags = small.tile([P, PAIR, ROW_TILES], BF16)
+                nc.gpsimd.tensor_scalar(
+                    out=flags[:].rearrange("p jj j -> p (jj j)"),
+                    in0=abs_sum_of[c][:],
+                    scalar1=0.0,
+                    scalar2=None,
+                    op0=ALU.is_gt,
+                )
+                num = psum_num.tile([P, ROW_TILES, PAIR], F32)
+                for i in range(ROW_TILES):
+                    near = [j for j in range(ROW_TILES) if abs(i - j) <= 1]
+                    for j in near:
+                        nc.tensor.matmul(
+                            num[:, i, :],
+                            lhsT=same_node[:, j].rearrange("p n s -> p (n s)")[:, i * P : (i + 1) * P],
+                            rhs=flags[:, :, j],
+                            start=(j == near[0]),
+                            stop=(j == near[-1]),
+                        )
+                square = small.tile([P, PAIR, ROW_TILES], F32)
+                nc.scalar.activation(
+                    out=square[:], in_=num[:].rearrange("p j jj -> p jj j"), func=ACT.Square, bias=-3.0
+                )
+                fac = small.tile([P, PAIR, ROW_TILES], F32)
+                nc.gpsimd.tensor_scalar(
+                    out=fac[:], in0=square[:], scalar1=2.0, scalar2=0.125, op0=ALU.add, op1=ALU.mult
+                )
+            else:
+                valid = small.tile([P, PAIR, SLOTS], F32)
+                nc.gpsimd.tensor_scalar(
+                    out=valid[:].rearrange("p j s -> p (j s)"),
+                    in0=abs_sum_of[c][:],
+                    scalar1=0.0,
+                    scalar2=None,
+                    op0=ALU.is_gt,
+                )
+                two = small.tile([P, PAIR, 1], F32)
+                nc.gpsimd.tensor_tensor(out=two[:], in0=valid[:, :, 0:1], in1=valid[:, :, 1:2], op=ALU.add)
+                num3 = small.tile([P, PAIR, 1], F32)
+                nc.gpsimd.tensor_tensor(out=num3[:], in0=two[:], in1=valid[:, :, 2:3], op=ALU.add)
+                less = small.tile([P, PAIR, 1], F32)
+                nc.gpsimd.tensor_scalar(out=less[:], in0=num3[:], scalar1=-3.0, scalar2=None, op0=ALU.add)
+                square3 = small.tile([P, PAIR, 1], F32)
+                nc.gpsimd.tensor_tensor(out=square3[:], in0=less[:], in1=less[:], op=ALU.mult)
+                fac = small.tile([P, PAIR, 1], F32)
+                nc.gpsimd.tensor_scalar(
+                    out=fac[:], in0=square3[:], scalar1=2.0, scalar2=1.0 / 6.0, op0=ALU.add, op1=ALU.mult
+                )
+            factor_of[c] = fac
+
+        def selection(c):
+            if by_rows(c):
+                sel = work.tile([P, PAIR * ROW_TILES, WIN], BF16)
+                nc.vector.tensor_tensor(
+                    out=sel[:],
+                    in0=window[:].rearrange("p jj j w -> p (jj j) w"),
+                    in1=factor_of[c][:]
+                    .rearrange("p jj j -> p (jj j)")
+                    .unsqueeze(2)
+                    .to_broadcast([P, PAIR * ROW_TILES, WIN]),
+                    op=ALU.mult,
+                )
+                select_of[c] = sel
 
         def sums(c):
             xs = xs_of[c]
-            xn = xn_of[c]
-            hid = work.tile([P, PAIR, K], BF16)
+            hid_src = work.tile([P, PAIR, D], BF16)
             s01 = work.tile([P, PAIR, D], F32)
-            n01 = work.tile([P, PAIR, D], F32)
-            nsum = work.tile([P, PAIR, D], F32)
             nc.vector.tensor_tensor(out=s01[:], in0=xs[:, :, 0:D], in1=xs[:, :, D : 2 * D], op=ALU.add)
-            nc.vector.tensor_tensor(out=n01[:], in0=xn[:, :, 0:D], in1=xn[:, :, D : 2 * D], op=ALU.add)
-            nc.vector.tensor_tensor(out=hid[:, :, 0:D], in0=s01[:], in1=xs[:, :, 2 * D : 3 * D], op=ALU.add)
-            nc.vector.tensor_tensor(out=nsum[:], in0=n01[:], in1=xn[:, :, 2 * D : 3 * D], op=ALU.add)
-            hid_of[c] = hid
-            nsum_of[c] = nsum
+            if not by_rows(c):
+                xn = xn_of[c][:].rearrange("p (j s) d -> p j s d", j=PAIR)
+                n01 = work.tile([P, PAIR, D], F32)
+                nsum = work.tile([P, PAIR, D], F32)
+                nc.vector.tensor_tensor(out=n01[:], in0=xn[:, :, 0, :], in1=xn[:, :, 1, :], op=ALU.add)
+                nc.vector.tensor_tensor(out=nsum[:], in0=n01[:], in1=xn[:, :, 2, :], op=ALU.add)
+                nsum_of[c] = nsum
+            nc.vector.tensor_tensor(out=hid_src[:], in0=s01[:], in1=xs[:, :, 2 * D : 3 * D], op=ALU.add)
+            hid_src_of[c] = hid_src
 
         def scale(c):
-            for j in range(PAIR):
-                nc.scalar.activation(
-                    out=hid_of[c][:, j, D:K], in_=nsum_of[c][:, j, :], func=ACT.Copy, scale=recip_of[c][:, j : j + 1]
-                )
+            if not by_rows(c):
+                hid_neigh = work.tile([P, PAIR, D], BF16)
+                for j in range(PAIR):
+                    nc.scalar.activation(
+                        out=hid_neigh[:, j, :], in_=nsum_of[c][:, j, :], func=ACT.Copy, scale=factor_of[c][:, j, :]
+                    )
+                hid_neigh_of[c] = hid_neigh
 
-        def transpose(c):
-            words = hid_of[c][:].rearrange("p j k -> p (j k)").bitcast(F32)
-            xts = []
+        def transpose_words(hid, xt):
+            words = hid[:].rearrange("p j k -> p (j k)").bitcast(F32)
             for j in range(PAIR):
-                xt = psum.tile([P, 2 * PASSES, P], F32)
-                for cu in range(2 * PASSES):
-                    g, u = divmod(cu, 2)
-                    first = j * (K // 2) + g * 2 * P
-                    nc.tensor.transpose(xt[:, cu, :], words[:, first + u : first + 2 * P : 2], ident[:])
-                xts.append(xt)
-            xt_of[c] = xts
+                for u in range(2):
+                    first = j * (D // 2) + u
+                    nc.tensor.transpose(xt[:, j, u, :], words[:, first : j * (D // 2) + D // 2 : 2], ident[:])
 
-        def regroup(c):
-            grouped = work.tile([P, PAIR * K], BF16, align_bytes=64)
+        def neighbours(c):
+            if by_rows(c):
+                nts = []
+                xn = xn_of[c]
+                sel = select_of[c]
+                for jj in range(PAIR):
+                    nt = psum_x.tile([P, PACK, P], F32, name="nt")
+                    for t in range(PACK):
+                        parts = [(0, 0, 43), (1, 42, 43), (1, 43, 86), (2, 85, 86), (2, 86, 128)]
+                        for n, (j, first, end) in enumerate(parts):
+                            k = jj * ROW_TILES + j
+                            nc.tensor.matmul(
+                                nt[:, t, first:end],
+                                lhsT=xn[:, k, t:D:PACK],
+                                rhs=sel[:, k, first - WIN_STEP * j : end - WIN_STEP * j],
+                                start=(n == 0),
+                                stop=(n == len(parts) - 1),
+                            )
+                    nts.append(nt)
+                nt_of[c] = nts
+            else:
+                nt = psum_x.tile([P, PAIR, 2, P], F32, name="nt")
+                transpose_words(hid_neigh_of[c], nt)
+                nt_of[c] = [nt]
+
+        def transposes(c):
+            xt = psum_x.tile([P, PAIR, 2, P], F32, name="xt")
+            transpose_words(hid_src_of[c], xt)
+            xt_of[c] = xt
+
+        def evacuate(c):
+            grouped = work.tile([P, PAIR * PASSES * P * PACK], BF16, align_bytes=64)
             grouped_w = grouped[:].bitcast(F32).rearrange("p (j g n u) -> p j g n u", j=PAIR, g=PASSES, u=2)
-            for j in range(PAIR):
-                nc.scalar.copy(out=grouped_w[:, j], in_=xt_of[c][j][:].rearrange("p (g u) n -> p g n u", u=2))
+            grouped_v = grouped[:].rearrange("p (j g n t) -> p j g n t", j=PAIR, g=PASSES, t=PACK)
+            nc.scalar.copy(out=grouped_w[:, :, 0], in_=xt_of[c][:].rearrange("p j u n -> p j n u"))
+            if by_rows(c):
+                for jj in range(PAIR):
+                    nc.scalar.activation(
+                        out=grouped_v[:, jj, 1],
+                        in_=nt_of[c][jj][:].rearrange("p t n -> p n t"),
+                        func=ACT.Copy,
+                        scale=8.0 / 6.0,
+                    )
+            else:
+                nc.scalar.copy(out=grouped_w[:, :, 1], in_=nt_of[c][0][:].rearrange("p j u n -> p j n u"))
             grouped_of[c] = grouped
 
         def quantise_and_multiply(c):
@@ -157,7 +279,7 @@ def tile_syntacticgcn_t_kernel(tc, src_node_features, neigh_node_features, W_map
             nc.vector.quantize_mx(out=codes[:].bitcast(FP8X4), scales=scales[:], in_=grouped_of[c][:])
             accs = []
             for j in range(PAIR):
-                acc = psum.tile([P, H], F32)
+                acc = psum_acc.tile([P, H], F32)
                 for g in range(PASSES):
                     cols = slice((j * PASSES + g) * P, (j * PASSES + g + 1) * P)
                     nc.tensor.matmul_mx(
@@ -181,26 +303,27 @@ def tile_syntacticgcn_t_kernel(tc, src_node_features, neigh_node_features, W_map
                 nc.vector.scalar_tensor_tensor(
                     out=result[:, j, :], in0=biased[:, j, :], scalar=SLOPE, in1=biased[:, j, :], op0=ALU.mult, op1=ALU.max
                 )
-            nc.sync.dma_start(out=out_v[:, PAIR * c : PAIR * (c + 1), :], in_=result[:])
+            nc.sync.dma_start(out=out_v[c], in_=result[:])
 
-        count(0)
-        reciprocal_count(0)
-        for i in range(N_PAIRS + 2):
-            if i + PREFETCH < N_PAIRS:
+        for i in range(-2, N_PAIRS + 2):
+            if PREFETCH <= i + PREFETCH < N_PAIRS:
                 load(i + PREFETCH)
-            if i + 1 < N_PAIRS:
-                count(i + 1)
-            if i < N_PAIRS:
-                sums(i)
-            if i + 1 < N_PAIRS:
-                reciprocal_count(i + 1)
-            if 0 <= i - 1 < N_PAIRS:
-                regroup(i - 1)
-            if i < N_PAIRS:
-                scale(i)
-            if 0 <= i - 2:
-                finish(i - 2)
+            if 0 <= i + 1 < N_PAIRS:
+                sums(i + 1)
+            if 0 <= i < N_PAIRS:
+                neighbours(i)
+                transposes(i)
             if 0 <= i - 1 < N_PAIRS:
                 quantise_and_multiply(i - 1)
-            if i < N_PAIRS:
-                transpose(i)
+            if 0 <= i + 1 < N_PAIRS:
+                selection(i + 1)
+            if 0 <= i + 2 < N_PAIRS:
+                count(i + 2)
+            if 0 <= i < N_PAIRS:
+                evacuate(i)
+            if 0 <= i + 1 < N_PAIRS:
+                scale(i + 1)
+            if 0 <= i + 2 < N_PAIRS:
+                factor(i + 2)
+            if 0 <= i - 2:
+                finish(i - 2)

@@ -8,6 +8,7 @@ U8 = mybir.dt.uint8
 FP8X4 = mybir.dt.float8_e4m3fn_x4
 ALU = mybir.AluOpType
 ACT = mybir.ActivationFunctionType
+AXIS = mybir.AxisListType
 
 P = 128
 SLOTS = 3
@@ -21,7 +22,7 @@ PACK = 4
 NODE_TILES = NODES // P
 PAIR = 2
 N_PAIRS = NODE_TILES // PAIR
-PREFETCH = 4
+PREFETCH = 5
 SLOPE = 0.01
 ROW_TILES = SLOTS
 WIN = 44
@@ -71,26 +72,36 @@ def tile_syntacticgcn_t_kernel(tc, src_node_features, neigh_node_features, W_map
         bias_bf = const.tile([P, H], BF16)
         nc.sync.dma_start(out=bias_bf[:], in_=b_map.partition_broadcast(P))
 
-        same_node = const.tile([P, ROW_TILES, P, SLOTS], BF16)
-        nc.gpsimd.memset(same_node[:], 1.0)
-        for j in range(ROW_TILES):
-            for low in (True, False):
-                sign = 1 if low else -1
-                nc.gpsimd.affine_select(
-                    out=same_node[:, j],
-                    in_=same_node[:, j],
-                    pattern=[[-SLOTS * sign, P], [0, SLOTS]],
-                    compare_op=ALU.is_ge,
-                    fill=0.0,
-                    base=P * j * sign + (0 if low else SLOTS - 1),
-                    channel_multiplier=sign,
-                )
-        window = const.tile([P, PAIR, ROW_TILES, WIN], BF16)
-        for jj in range(PAIR):
-            for j in range(ROW_TILES):
-                nc.gpsimd.tensor_copy(out=window[:, jj, j, :], in_=same_node[:, j, WIN_STEP * j : WIN_STEP * j + WIN, 0])
         ident = const.tile([P, P], F32)
         make_identity(nc, ident[:])
+        window = const.tile([P, ROW_TILES, WIN], BF16)
+        nc.gpsimd.memset(window[:], 1.0)
+        for sign, base in ((1, 0), (-1, SLOTS - 1)):
+            nc.gpsimd.affine_select(
+                out=window[:],
+                in_=window[:],
+                pattern=[[2 * sign, ROW_TILES], [-SLOTS * sign, WIN]],
+                compare_op=ALU.is_ge,
+                fill=0.0,
+                base=base,
+                channel_multiplier=sign,
+            )
+        same_node = const.tile([P, ROW_TILES, P, SLOTS], BF16)
+        nc.vector.memset(same_node[:], 0.0)
+        for j in range(ROW_TILES):
+            nc.vector.tensor_copy(
+                out=same_node[:, j, WIN_STEP * j : WIN_STEP * j + WIN, :],
+                in_=window[:, j, :].unsqueeze(2).to_broadcast([P, WIN, SLOTS]),
+            )
+        window8 = const.tile([P, PAIR, ROW_TILES * WIN], BF16)
+        for jj in range(PAIR):
+            nc.vector.tensor_scalar(
+                out=window8[:, jj, :],
+                in0=window[:].rearrange("p j w -> p (j w)"),
+                scalar1=0.125,
+                scalar2=None,
+                op0=ALU.mult,
+            )
 
         w_grouped = const.tile([P, PASSES * H * PACK], BF16, align_bytes=64)
         w_codes = const.tile([P, PASSES * H], U32, align_bytes=64)
@@ -110,6 +121,8 @@ def tile_syntacticgcn_t_kernel(tc, src_node_features, neigh_node_features, W_map
         nc.vector.tensor_copy(out=bias[:], in_=bias_bf[:])
 
         abs_sum_of = {}
+        num_of = {}
+        square_of = {}
         factor_of = {}
         select_of = {}
         hid_src_of = {}
@@ -129,16 +142,12 @@ def tile_syntacticgcn_t_kernel(tc, src_node_features, neigh_node_features, W_map
                 )
             abs_sum_of[c] = abs_sum
 
-        def factor(c):
+        def number(c):
+            flags = small.tile([P, PAIR, SLOTS], BF16)
+            nc.scalar.activation(
+                out=flags[:].rearrange("p j s -> p (j s)"), in_=abs_sum_of[c][:], func=ACT.Sign
+            )
             if by_rows(c):
-                flags = small.tile([P, PAIR, ROW_TILES], BF16)
-                nc.gpsimd.tensor_scalar(
-                    out=flags[:].rearrange("p jj j -> p (jj j)"),
-                    in0=abs_sum_of[c][:],
-                    scalar1=0.0,
-                    scalar2=None,
-                    op0=ALU.is_gt,
-                )
                 num = psum_num.tile([P, ROW_TILES, PAIR], F32)
                 for i in range(ROW_TILES):
                     near = [j for j in range(ROW_TILES) if abs(i - j) <= 1]
@@ -150,50 +159,39 @@ def tile_syntacticgcn_t_kernel(tc, src_node_features, neigh_node_features, W_map
                             start=(j == near[0]),
                             stop=(j == near[-1]),
                         )
-                square = small.tile([P, PAIR, ROW_TILES], F32)
-                nc.scalar.activation(
-                    out=square[:], in_=num[:].rearrange("p j jj -> p jj j"), func=ACT.Square, bias=-3.0
-                )
-                fac = small.tile([P, PAIR, ROW_TILES], F32)
-                nc.gpsimd.tensor_scalar(
-                    out=fac[:], in0=square[:], scalar1=2.0, scalar2=0.125, op0=ALU.add, op1=ALU.mult
-                )
+                num_of[c] = num[:].rearrange("p j jj -> p jj j")
             else:
-                valid = small.tile([P, PAIR, SLOTS], F32)
-                nc.gpsimd.tensor_scalar(
-                    out=valid[:].rearrange("p j s -> p (j s)"),
-                    in0=abs_sum_of[c][:],
-                    scalar1=0.0,
-                    scalar2=None,
-                    op0=ALU.is_gt,
-                )
-                two = small.tile([P, PAIR, 1], F32)
-                nc.gpsimd.tensor_tensor(out=two[:], in0=valid[:, :, 0:1], in1=valid[:, :, 1:2], op=ALU.add)
                 num3 = small.tile([P, PAIR, 1], F32)
-                nc.gpsimd.tensor_tensor(out=num3[:], in0=two[:], in1=valid[:, :, 2:3], op=ALU.add)
-                less = small.tile([P, PAIR, 1], F32)
-                nc.gpsimd.tensor_scalar(out=less[:], in0=num3[:], scalar1=-3.0, scalar2=None, op0=ALU.add)
-                square3 = small.tile([P, PAIR, 1], F32)
-                nc.gpsimd.tensor_tensor(out=square3[:], in0=less[:], in1=less[:], op=ALU.mult)
-                fac = small.tile([P, PAIR, 1], F32)
-                nc.gpsimd.tensor_scalar(
-                    out=fac[:], in0=square3[:], scalar1=2.0, scalar2=1.0 / 6.0, op0=ALU.add, op1=ALU.mult
-                )
-            factor_of[c] = fac
+                nc.vector.tensor_reduce(out=num3[:, :, 0], in_=flags[:], axis=AXIS.X, op=ALU.add)
+                num_of[c] = num3[:]
+
+        def square(c):
+            width = ROW_TILES if by_rows(c) else 1
+            sq = small.tile([P, PAIR, width], F32)
+            nc.scalar.activation(out=sq[:], in_=num_of[c], func=ACT.Square, bias=-3.0)
+            square_of[c] = sq
 
         def selection(c):
             if by_rows(c):
                 sel = work.tile([P, PAIR * ROW_TILES, WIN], BF16)
-                nc.vector.tensor_tensor(
+                nc.vector.scalar_tensor_tensor(
                     out=sel[:],
-                    in0=window[:].rearrange("p jj j w -> p (jj j) w"),
-                    in1=factor_of[c][:]
+                    in0=square_of[c][:]
                     .rearrange("p jj j -> p (jj j)")
                     .unsqueeze(2)
                     .to_broadcast([P, PAIR * ROW_TILES, WIN]),
-                    op=ALU.mult,
+                    scalar=2.0,
+                    in1=window8[:].rearrange("p jj (j w) -> p (jj j) w", w=WIN),
+                    op0=ALU.add,
+                    op1=ALU.mult,
                 )
                 select_of[c] = sel
+            else:
+                fac = small.tile([P, PAIR, 1], F32)
+                nc.vector.tensor_scalar(
+                    out=fac[:], in0=square_of[c][:], scalar1=2.0, scalar2=1.0 / 6.0, op0=ALU.add, op1=ALU.mult
+                )
+                factor_of[c] = fac
 
         def sums(c):
             xs = xs_of[c]
@@ -305,7 +303,7 @@ def tile_syntacticgcn_t_kernel(tc, src_node_features, neigh_node_features, W_map
                 )
             nc.sync.dma_start(out=out_v[c], in_=result[:])
 
-        for i in range(-2, N_PAIRS + 2):
+        for i in range(-3, N_PAIRS + 2):
             if PREFETCH <= i + PREFETCH < N_PAIRS:
                 load(i + PREFETCH)
             if 0 <= i + 1 < N_PAIRS:
@@ -317,13 +315,15 @@ def tile_syntacticgcn_t_kernel(tc, src_node_features, neigh_node_features, W_map
                 quantise_and_multiply(i - 1)
             if 0 <= i + 1 < N_PAIRS:
                 selection(i + 1)
-            if 0 <= i + 2 < N_PAIRS:
-                count(i + 2)
+            if 0 <= i + 3 < N_PAIRS:
+                count(i + 3)
             if 0 <= i < N_PAIRS:
                 evacuate(i)
             if 0 <= i + 1 < N_PAIRS:
                 scale(i + 1)
             if 0 <= i + 2 < N_PAIRS:
-                factor(i + 2)
+                square(i + 2)
+            if 0 <= i + 3 < N_PAIRS:
+                number(i + 3)
             if 0 <= i - 2:
                 finish(i - 2)

@@ -69,8 +69,8 @@ def tile_syntacticgcn_t_kernel(tc, src_node_features, neigh_node_features, W_map
         )
         for c in range(1, PREFETCH):
             load(c)
-        bias_bf = const.tile([P, H], BF16)
-        nc.sync.dma_start(out=bias_bf[:], in_=b_map.partition_broadcast(P))
+        bias = const.tile([P, H], BF16)
+        nc.sync.dma_start(out=bias[:], in_=b_map.partition_broadcast(P))
 
         ident = const.tile([P, P], F32)
         make_identity(nc, ident[:])
@@ -117,8 +117,6 @@ def tile_syntacticgcn_t_kernel(tc, src_node_features, neigh_node_features, W_map
                 scales=w_scales[:, g * H : (g + 1) * H],
                 in_=w_grouped[:, g * 4 * H : (g + 1) * 4 * H],
             )
-        bias = const.tile([P, H], F32)
-        nc.vector.tensor_copy(out=bias[:], in_=bias_bf[:])
 
         abs_sum_of = {}
         num_of = {}
@@ -197,16 +195,19 @@ def tile_syntacticgcn_t_kernel(tc, src_node_features, neigh_node_features, W_map
             xs = xs_of[c]
             hid_src = work.tile([P, PAIR, D], BF16)
             s01 = work.tile([P, PAIR, D], F32)
-            nc.vector.tensor_tensor(out=s01[:], in0=xs[:, :, 0:D], in1=xs[:, :, D : 2 * D], op=ALU.add)
+            for j in range(PAIR):
+                nc.vector.tensor_tensor(out=s01[:, j], in0=xs[:, j, 0:D], in1=xs[:, j, D : 2 * D], op=ALU.add)
             if not by_rows(c):
                 xn = xn_of[c][:].rearrange("p (j s) d -> p j s d", j=PAIR)
                 n01 = work.tile([P, PAIR, D], F32)
-                nsum = work.tile([P, PAIR, D], F32)
                 nc.vector.tensor_tensor(out=n01[:], in0=xn[:, :, 0, :], in1=xn[:, :, 1, :], op=ALU.add)
+            for j in range(PAIR):
+                nc.vector.tensor_tensor(out=hid_src[:, j], in0=s01[:, j], in1=xs[:, j, 2 * D : 3 * D], op=ALU.add)
+            hid_src_of[c] = hid_src
+            if not by_rows(c):
+                nsum = work.tile([P, PAIR, D], F32)
                 nc.vector.tensor_tensor(out=nsum[:], in0=n01[:], in1=xn[:, :, 2, :], op=ALU.add)
                 nsum_of[c] = nsum
-            nc.vector.tensor_tensor(out=hid_src[:], in0=s01[:], in1=xs[:, :, 2 * D : 3 * D], op=ALU.add)
-            hid_src_of[c] = hid_src
 
         def scale(c):
             if not by_rows(c):

import concourse.mybir as mybir
from concourse.masks import make_identity

F32 = mybir.dt.float32
BF16 = mybir.dt.bfloat16
U32 = mybir.dt.uint32
U8 = mybir.dt.uint8
FP8X4 = mybir.dt.float8_e4m3fn_x4
ALU = mybir.AluOpType
ACT = mybir.ActivationFunctionType
AXIS = mybir.AxisListType

P = 128
SLOTS = 3
D = 512
H = 512
K = 2 * D
NODES = 4096
K_PASS = 512
PASSES = K // K_PASS
PACK = 4
NODE_TILES = NODES // P
PAIR = 2
N_PAIRS = NODE_TILES // PAIR
PREFETCH = 5
SLOPE = 0.01
ROW_TILES = SLOTS
WIN = 44
WIN_STEP = 42

FLOPS = 2 * NODES * K * H


def tile_syntacticgcn_t_kernel(tc, src_node_features, neigh_node_features, W_map, b_map, out):
    nc = tc.nc

    src_v = src_node_features.rearrange("b q m d -> (b q) (m d)").rearrange("(c j p) x -> c p j x", j=PAIR, p=P)
    neigh_v = neigh_node_features.rearrange("b q m d -> (b q) (m d)").rearrange("(c j p) x -> c p j x", j=PAIR, p=P)
    rows_v = neigh_node_features.rearrange("b q m d -> (b q m) d").rearrange("(c k p) d -> c p k d", k=PAIR * ROW_TILES, p=P)
    out_v = out.rearrange("(c j p) h -> c p j h", j=PAIR, p=P)

    def by_rows(c):
        return c % 4 != 2

    with tc.tile_pool(name="const", bufs=1) as const, tc.tile_pool(name="data", bufs=PREFETCH + 1) as data, tc.tile_pool(
        name="work", bufs=2
    ) as work, tc.tile_pool(name="small", bufs=3) as small, tc.tile_pool(name="junk", bufs=4) as junk_pool, tc.psum_pool(
        name="psum_x", bufs=2
    ) as psum_x, tc.psum_pool(name="psum_acc", bufs=3) as psum_acc, tc.psum_pool(name="psum_num", bufs=1) as psum_num:
        xs_of = {}
        xn_of = {}

        def load(c):
            xn = data.tile([P, PAIR * SLOTS, D], BF16)
            if by_rows(c):
                nc.sync.dma_start(out=xn[:], in_=rows_v[c])
            else:
                nc.sync.dma_start(out=xn[:].rearrange("p (j s) d -> p j (s d)", j=PAIR), in_=neigh_v[c])
            xs = data.tile([P, PAIR, SLOTS * D], BF16)
            nc.sync.dma_start(out=xs[:], in_=src_v[c])
            xn_of[c] = xn
            xs_of[c] = xs

        load(0)
        w_raw = const.tile([P, PASSES * PACK * H], BF16)
        nc.sync.dma_start(
            out=w_raw[:].rearrange("p (g th) -> p g th", g=PASSES),
            in_=W_map.rearrange("(g q t) h -> q g (t h)", g=PASSES, t=PACK),
        )
        for c in range(1, PREFETCH):
            load(c)
        bias = const.tile([P, H], BF16)
        nc.sync.dma_start(out=bias[:], in_=b_map.partition_broadcast(P))

        ident = const.tile([P, P], F32)
        make_identity(nc, ident[:])
        window = const.tile([P, ROW_TILES, WIN], BF16)
        nc.gpsimd.memset(window[:], 1.0)
        for sign, base in ((1, 0), (-1, SLOTS - 1)):
            nc.gpsimd.affine_select(
                out=window[:],
                in_=window[:],
                pattern=[[2 * sign, ROW_TILES], [-SLOTS * sign, WIN]],
                compare_op=ALU.is_ge,
                fill=0.0,
                base=base,
                channel_multiplier=sign,
            )
        same_node = const.tile([P, ROW_TILES, P, SLOTS], BF16)
        nc.vector.memset(same_node[:], 0.0)
        for j in range(ROW_TILES):
            nc.vector.tensor_copy(
                out=same_node[:, j, WIN_STEP * j : WIN_STEP * j + WIN, :],
                in_=window[:, j, :].unsqueeze(2).to_broadcast([P, WIN, SLOTS]),
            )
        window8 = const.tile([P, PAIR, ROW_TILES * WIN], BF16)
        for jj in range(PAIR):
            nc.vector.tensor_scalar(
                out=window8[:, jj, :],
                in0=window[:].rearrange("p j w -> p (j w)"),
                scalar1=0.125,
                scalar2=None,
                op0=ALU.mult,
            )

        w_grouped = const.tile([P, PASSES * H * PACK], BF16, align_bytes=64)
        w_codes = const.tile([P, PASSES * H], U32, align_bytes=64)
        w_scales = const.tile([P, PASSES * H], U8, align_bytes=64)
        for g in range(PASSES):
            nc.vector.tensor_copy(
                out=w_grouped[:, g * 4 * H : (g + 1) * 4 * H].rearrange("p (h t) -> p h t", t=PACK),
                in_=w_raw[:, g * 4 * H : (g + 1) * 4 * H].rearrange("p (t h) -> p h t", t=PACK),
            )
        for g in range(PASSES):
            nc.vector.quantize_mx(
                out=w_codes[:, g * H : (g + 1) * H].bitcast(FP8X4),
                scales=w_scales[:, g * H : (g + 1) * H],
                in_=w_grouped[:, g * 4 * H : (g + 1) * 4 * H],
            )

        abs_sum_of = {}
        num_of = {}
        square_of = {}
        factor_of = {}
        select_of = {}
        hid_src_of = {}
        nsum_of = {}
        hid_neigh_of = {}
        xt_of = {}
        nt_of = {}
        grouped_of = {}
        acc_of = {}

        def count(c):
            abs_sum = small.tile([P, PAIR * SLOTS], F32)
            for k in range(PAIR * SLOTS):
                junk = junk_pool.tile([P, D], BF16)
                nc.scalar.activation(
                    out=junk[:], in_=xn_of[c][:, k, :], func=ACT.Abs, accum_out=abs_sum[:, k : k + 1]
                )
            abs_sum_of[c] = abs_sum

        def number(c):
            flags = small.tile([P, PAIR, SLOTS], BF16)
            nc.scalar.activation(
                out=flags[:].rearrange("p j s -> p (j s)"), in_=abs_sum_of[c][:], func=ACT.Sign
            )
            if by_rows(c):
                num = psum_num.tile([P, ROW_TILES, PAIR], F32)
                for i in range(ROW_TILES):
                    near = [j for j in range(ROW_TILES) if abs(i - j) <= 1]
                    for j in near:
                        nc.tensor.matmul(
                            num[:, i, :],
                            lhsT=same_node[:, j].rearrange("p n s -> p (n s)")[:, i * P : (i + 1) * P],
                            rhs=flags[:, :, j],
                            start=(j == near[0]),
                            stop=(j == near[-1]),
                        )
                num_of[c] = num[:].rearrange("p j jj -> p jj j")
            else:
                num3 = small.tile([P, PAIR, 1], F32)
                nc.vector.tensor_reduce(out=num3[:, :, 0], in_=flags[:], axis=AXIS.X, op=ALU.add)
                num_of[c] = num3[:]

        def square(c):
            width = ROW_TILES if by_rows(c) else 1
            sq = small.tile([P, PAIR, width], F32)
            nc.scalar.activation(out=sq[:], in_=num_of[c], func=ACT.Square, bias=-3.0)
            square_of[c] = sq

        def selection(c):
            if by_rows(c):
                sel = work.tile([P, PAIR * ROW_TILES, WIN], BF16)
                nc.vector.scalar_tensor_tensor(
                    out=sel[:],
                    in0=square_of[c][:]
                    .rearrange("p jj j -> p (jj j)")
                    .unsqueeze(2)
                    .to_broadcast([P, PAIR * ROW_TILES, WIN]),
                    scalar=2.0,
                    in1=window8[:].rearrange("p jj (j w) -> p (jj j) w", w=WIN),
                    op0=ALU.add,
                    op1=ALU.mult,
                )
                select_of[c] = sel
            else:
                fac = small.tile([P, PAIR, 1], F32)
                nc.vector.tensor_scalar(
                    out=fac[:], in0=square_of[c][:], scalar1=2.0, scalar2=1.0 / 6.0, op0=ALU.add, op1=ALU.mult
                )
                factor_of[c] = fac

        def sums(c):
            xs = xs_of[c]
            hid_src = work.tile([P, PAIR, D], BF16)
            s01 = work.tile([P, PAIR, D], F32)
            for j in range(PAIR):
                nc.vector.tensor_tensor(out=s01[:, j], in0=xs[:, j, 0:D], in1=xs[:, j, D : 2 * D], op=ALU.add)
            if not by_rows(c):
                xn = xn_of[c][:].rearrange("p (j s) d -> p j s d", j=PAIR)
                n01 = work.tile([P, PAIR, D], F32)
                nc.vector.tensor_tensor(out=n01[:], in0=xn[:, :, 0, :], in1=xn[:, :, 1, :], op=ALU.add)
            for j in range(PAIR):
                nc.vector.tensor_tensor(out=hid_src[:, j], in0=s01[:, j], in1=xs[:, j, 2 * D : 3 * D], op=ALU.add)
            hid_src_of[c] = hid_src
            if not by_rows(c):
                nsum = work.tile([P, PAIR, D], F32)
                nc.vector.tensor_tensor(out=nsum[:], in0=n01[:], in1=xn[:, :, 2, :], op=ALU.add)
                nsum_of[c] = nsum

        def scale(c):
            if not by_rows(c):
                hid_neigh = work.tile([P, PAIR, D], BF16)
                for j in range(PAIR):
                    nc.scalar.activation(
                        out=hid_neigh[:, j, :], in_=nsum_of[c][:, j, :], func=ACT.Copy, scale=factor_of[c][:, j, :]
                    )
                hid_neigh_of[c] = hid_neigh

        def transpose_words(hid, xt):
            words = hid[:].rearrange("p j k -> p (j k)").bitcast(F32)
            for j in range(PAIR):
                for u in range(2):
                    first = j * (D // 2) + u
                    nc.tensor.transpose(xt[:, j, u, :], words[:, first : j * (D // 2) + D // 2 : 2], ident[:])

        def neighbours(c):
            if by_rows(c):
                nts = []
                xn = xn_of[c]
                sel = select_of[c]
                for jj in range(PAIR):
                    nt = psum_x.tile([P, PACK, P], F32, name="nt")
                    for t in range(PACK):
                        parts = [(0, 0, 43), (1, 42, 43), (1, 43, 86), (2, 85, 86), (2, 86, 128)]
                        for n, (j, first, end) in enumerate(parts):
                            k = jj * ROW_TILES + j
                            nc.tensor.matmul(
                                nt[:, t, first:end],
                                lhsT=xn[:, k, t:D:PACK],
                                rhs=sel[:, k, first - WIN_STEP * j : end - WIN_STEP * j],
                                start=(n == 0),
                                stop=(n == len(parts) - 1),
                            )
                    nts.append(nt)
                nt_of[c] = nts
            else:
                nt = psum_x.tile([P, PAIR, 2, P], F32, name="nt")
                transpose_words(hid_neigh_of[c], nt)
                nt_of[c] = [nt]

        def transposes(c):
            xt = psum_x.tile([P, PAIR, 2, P], F32, name="xt")
            transpose_words(hid_src_of[c], xt)
            xt_of[c] = xt

        def evacuate(c):
            grouped = work.tile([P, PAIR * PASSES * P * PACK], BF16, align_bytes=64)
            grouped_w = grouped[:].bitcast(F32).rearrange("p (j g n u) -> p j g n u", j=PAIR, g=PASSES, u=2)
            grouped_v = grouped[:].rearrange("p (j g n t) -> p j g n t", j=PAIR, g=PASSES, t=PACK)
            nc.scalar.copy(out=grouped_w[:, :, 0], in_=xt_of[c][:].rearrange("p j u n -> p j n u"))
            if by_rows(c):
                for jj in range(PAIR):
                    nc.scalar.activation(
                        out=grouped_v[:, jj, 1],
                        in_=nt_of[c][jj][:].rearrange("p t n -> p n t"),
                        func=ACT.Copy,
                        scale=8.0 / 6.0,
                    )
            else:
                nc.scalar.copy(out=grouped_w[:, :, 1], in_=nt_of[c][0][:].rearrange("p j u n -> p j n u"))
            grouped_of[c] = grouped

        def quantise_and_multiply(c):
            codes = work.tile([P, PAIR * PASSES * P], U32, align_bytes=64)
            scales = work.tile([P, PAIR * PASSES * P], U8, align_bytes=64)
            nc.vector.quantize_mx(out=codes[:].bitcast(FP8X4), scales=scales[:], in_=grouped_of[c][:])
            accs = []
            for j in range(PAIR):
                acc = psum_acc.tile([P, H], F32)
                for g in range(PASSES):
                    cols = slice((j * PASSES + g) * P, (j * PASSES + g + 1) * P)
                    nc.tensor.matmul_mx(
                        out=acc[:],
                        lhsT=codes[:, cols].bitcast(FP8X4),
                        lhsT_scale=scales[:, cols],
                        rhs=w_codes[:, g * H : (g + 1) * H].bitcast(FP8X4),
                        rhs_scale=w_scales[:, g * H : (g + 1) * H],
                        start=(g == 0),
                        stop=(g == PASSES - 1),
                    )
                accs.append(acc)
            acc_of[c] = accs

        def finish(c):
            biased = work.tile([P, PAIR, H], F32)
            result = work.tile([P, PAIR, H], F32)
            for j in range(PAIR):
                nc.vector.tensor_tensor(out=biased[:, j, :], in0=acc_of[c][j][:], in1=bias[:], op=ALU.add)
            for j in range(PAIR):
                nc.vector.scalar_tensor_tensor(
                    out=result[:, j, :], in0=biased[:, j, :], scalar=SLOPE, in1=biased[:, j, :], op0=ALU.mult, op1=ALU.max
                )
            nc.sync.dma_start(out=out_v[c], in_=result[:])

        for i in range(-3, N_PAIRS + 2):
            if PREFETCH <= i + PREFETCH < N_PAIRS:
                load(i + PREFETCH)
            if 0 <= i + 1 < N_PAIRS:
                sums(i + 1)
            if 0 <= i < N_PAIRS:
                neighbours(i)
                transposes(i)
            if 0 <= i - 1 < N_PAIRS:
                quantise_and_multiply(i - 1)
            if 0 <= i + 1 < N_PAIRS:
                selection(i + 1)
            if 0 <= i + 3 < N_PAIRS:
                count(i + 3)
            if 0 <= i < N_PAIRS:
                evacuate(i)
            if 0 <= i + 1 < N_PAIRS:
                scale(i + 1)
            if 0 <= i + 2 < N_PAIRS:
                square(i + 2)
            if 0 <= i + 3 < N_PAIRS:
                number(i + 3)
            if 0 <= i - 2:
                finish(i - 2)
